import numpy as np
import ml_dtypes


def mxq(x, axis, fmt="e4m3"):
    dtype, down = {"e4m3": (ml_dtypes.float8_e4m3fn, 7), "e5m2": (ml_dtypes.float8_e5m2, 14)}[fmt]
    v = np.moveaxis(np.asarray(x, np.float32).astype(ml_dtypes.bfloat16).astype(np.float64), axis, -1)
    blocks = v.reshape(v.shape[:-1] + (-1, 32))
    amax = np.abs(blocks).max(-1, keepdims=True)
    byte = np.maximum(np.where(amax > 0, np.frexp(amax)[1] - 1 + 127, 0) - down, 1)
    scale = np.exp2(byte - 127.0)
    codes = (blocks / scale).astype(np.float32).astype(dtype).astype(np.float64)
    return np.moveaxis((codes * scale).reshape(v.shape), -1, axis)


WIDE = False


def mx_kscale(k):
    if not WIDE:
        return np.ones(k)
    levels = np.array([10, -10, 5, -5, 0])
    if k % 512:
        return np.exp2(np.random.permutation(np.resize(levels, k // 32))).repeat(32)
    a = np.empty((k // 512, 16))
    for p in range(k // 512):
        a[p, :8] = np.random.permutation(np.resize(levels, 8))
        for g in range(8):
            far = levels[np.abs(levels - a[p, g]) >= 10]
            a[p, g + 8] = far[np.random.randint(len(far))]
    return np.exp2(a.ravel()).repeat(32)


BF16 = ml_dtypes.bfloat16


def bf(x):
    return np.asarray(x, np.float32).astype(BF16)


def f64(x):
    return np.asarray(x).astype(np.float64)


E2M1 = np.array([0.0, 0.5, 1.0, 1.5, 2.0, 3.0, 4.0, 6.0, -0.0, -0.5, -1.0, -1.5, -2.0, -3.0, -4.0, -6.0])


def pack_weight(w, fmt):
    k, n = w.shape
    w = f64(bf(w)).reshape(k // 32, 32, n)
    amax = np.abs(w).max(1)
    if fmt == "e4m3":
        byte = np.frexp(amax)[1] - 1 + 127 - 7
    else:
        mant, ex = np.frexp(amax / 6.0)
        byte = np.where(mant > 0.5, ex, ex - 1) + 127
    byte = np.clip(np.where(amax > 0, byte, 1), 1, 254)
    scaled = (w * np.exp2(127.0 - byte)[:, None, :]).reshape(k, n).astype(np.float32)
    by_word = np.ascontiguousarray(scaled.reshape(k // 512, 128, 4, n).transpose(0, 1, 3, 2))
    if fmt == "e4m3":
        words = by_word.astype(ml_dtypes.float8_e4m3fn).view(np.uint8)
    else:
        c = by_word.astype(ml_dtypes.float4_e2m1fn).view(np.uint8) & 0xF
        words = c[..., 0::2] | (c[..., 1::2] << 4)
    return np.ascontiguousarray(words), np.ascontiguousarray(byte.astype(np.uint8).reshape(k // 512, 16, n))


def unpack_weight(words, scales, fmt):
    g, p, n, _ = words.shape
    if fmt == "e4m3":
        vals = np.ascontiguousarray(words).view(ml_dtypes.float8_e4m3fn).astype(np.float64)
    else:
        nib = np.empty((g, p, n, 4), np.uint8)
        nib[..., 0::2] = words & 0xF
        nib[..., 1::2] = words >> 4
        vals = E2M1[nib]
    vals = vals * np.repeat(np.exp2(scales.astype(np.float64) - 127.0), 8, axis=1)[..., None]
    return vals.transpose(0, 1, 3, 2).reshape(g * 512, n)


B, L, D = 3, 512, 512
SIG = 2.0
FMT = "e4m3"


def setup_inputs():
    s, t = mx_kscale(D), mx_kscale(D)
    x1 = bf(np.random.standard_normal((B, L, D)) * s)
    words, scales = pack_weight(np.random.standard_normal((D, D)) * SIG / D / s[:, None] * t, FMT)
    x2 = bf(np.random.standard_normal((B, L, D)) / t)
    return {"x1": x1,
            "bi_linear_w_words": words,
            "bi_linear_w_scales": scales,
            "x2": x2}


def reference(x1, bi_linear_w_words, bi_linear_w_scales, x2):
    h = mxq(f64(x1), 2, "e4m3") @ unpack_weight(bi_linear_w_words, bi_linear_w_scales, FMT)
    return mxq(h, 2, "e4m3") @ mxq(f64(x2), 2, "e4m3").transpose(0, 2, 1)

@@ -1,0 +1,182 @@
+from contextlib import ExitStack
+
+import concourse.mybir as mybir
+from concourse.masks import make_identity
+
+BF16 = mybir.dt.bfloat16
+F32 = mybir.dt.float32
+I32 = mybir.dt.int32
+U32 = mybir.dt.uint32
+U8 = mybir.dt.uint8
+FP8X4 = mybir.dt.float8_e4m3fn_x4
+
+B, L, D = 3, 512, 512
+P = 128
+PACK = 4
+CHUNKS = L // P
+HALF = L // 2
+HALVES = L // HALF
+PLANES = 2
+WORDS = D // 2
+QUADRANT = 32
+SCALE_ROWS = 4
+
+TRANSPOSE_BANKS = 3
+PRODUCT_BANKS = 5
+
+FLOPS = 2 * B * L * D * D + 2 * B * L * L * D
+
+
+def tile_coattentionandcombine_pa_kernel(
+    tc, x1, bi_linear_w_words, bi_linear_w_scales, x2, out
+):
+    nc = tc.nc
+    with ExitStack() as ctx:
+        fixed = ctx.enter_context(tc.tile_pool(name="fixed", bufs=1))
+        per_batch = ctx.enter_context(tc.tile_pool(name="per_batch", bufs=B))
+        transposed = ctx.enter_context(tc.psum_pool(name="transposed", bufs=TRANSPOSE_BANKS))
+        products = ctx.enter_context(tc.psum_pool(name="products", bufs=PRODUCT_BANKS))
+        ctx.enter_context(tc.manual_schedule())
+
+        def copy_out_of_psum(on_vector, out_, in_):
+            if on_vector:
+                nc.vector.tensor_copy(out=out_, in_=in_)
+            else:
+                nc.scalar.copy(out=out_, in_=in_)
+
+        def quantise(operand, cols):
+            nc.vector.quantize_mx(
+                out=operand["codes"][:, cols].bitcast(FP8X4),
+                scales=operand["scales"][:, cols],
+                in_=operand["grouped"][:, cols, :].rearrange("p l s -> p (l s)"),
+            )
+
+        w_scales_in = fixed.tile([P, D], U8, align_bytes=64)
+        nc.vector.memset(w_scales_in[:].bitcast(I32), 0)
+        w_codes_in = fixed.tile([P, D], I32, align_bytes=64)
+        w_scales = fixed.tile([P, PACK, P], U8, align_bytes=64)
+        w_codes = fixed.tile([P, PACK, P], I32, align_bytes=64)
+        ident_f32 = fixed.tile([P, P], F32)
+        make_identity(nc, ident_f32[:])
+
+        x1_rows, x2_rows, x1_q, x2_q, h_q, sim_rows = [], [], [], [], [], []
+        for b in range(B):
+            for rows_of, name in ((x1_rows, "x1_rows"), (x2_rows, "x2_rows")):
+                rows = per_batch.tile([P, CHUNKS, D], BF16, tag=name)
+                rows_of.append(rows)
+            for operands, name in ((x1_q, "x1"), (x2_q, "x2"), (h_q, "h")):
+                grouped = per_batch.tile([P, L, PACK], BF16, align_bytes=64, tag=name + "_grouped")
+                codes = per_batch.tile([P, L], U32, align_bytes=64, tag=name + "_codes")
+                scales = per_batch.tile([P, L], U8, align_bytes=64, tag=name + "_scales")
+                operands.append({"grouped": grouped, "codes": codes, "scales": scales})
+            result = per_batch.tile([P, CHUNKS, L], F32, tag="sim_rows")
+            sim_rows.append(result)
+
+        def load(tile, tensor, b, pieces):
+            rows = tensor[b].rearrange("(p a) d -> p a d", a=CHUNKS)
+            step = CHUNKS // pieces
+            for a in range(0, CHUNKS, step):
+                nc.sync.dma_start(out=tile[:, a : a + step, :], in_=rows[:, a : a + step, :])
+
+        load(x1_rows[0], x1, 0, HALVES)
+        for q in range(P // QUADRANT):
+            nc.sync.dma_start(
+                out=w_scales_in[QUADRANT * q : QUADRANT * q + SCALE_ROWS, :].bitcast(I32),
+                in_=bi_linear_w_scales[0, SCALE_ROWS * q : SCALE_ROWS * (q + 1), :].bitcast(I32),
+            )
+        nc.sync.dma_start(
+            out=w_codes_in[:], in_=bi_linear_w_words[0].rearrange("p n t -> p (n t)").bitcast(I32)
+        )
+        load(x1_rows[1], x1, 1, 1)
+        load(x2_rows[0], x2, 0, 1)
+        load(x2_rows[1], x2, 1, 1)
+        load(x1_rows[2], x1, 2, 1)
+        load(x2_rows[2], x2, 2, 1)
+
+
+        def reorder_w():
+            nc.vector.tensor_copy(out=w_codes[:], in_=w_codes_in[:].rearrange("p (m s) -> p s m", s=PACK))
+            nc.vector.tensor_copy(out=w_scales[:], in_=w_scales_in[:].rearrange("p (m s) -> p s m", s=PACK))
+
+        def prepare(rows, operand):
+            banks = []
+            for half in range(HALVES):
+                x_t = transposed.tile([P, PLANES, HALF], F32, tag="t")
+                for a in range(HALF // P):
+                    words = rows[:, HALF // P * half + a, :].bitcast(F32)
+                    for u in range(PLANES):
+                        nc.tensor.transpose(
+                            x_t[:, u, P * a : P * (a + 1)], words[:, u:WORDS:PLANES], ident_f32[:]
+                        )
+                banks.append(x_t)
+            for half in range(HALVES):
+                copy_out_of_psum(
+                    half == 1,
+                    operand["grouped"][:, HALF * half : HALF * (half + 1), :].bitcast(F32),
+                    banks[half][:].rearrange("p u l -> p l u"),
+                )
+            for half in range(HALVES):
+                quantise(operand, slice(HALF * half, HALF * (half + 1)))
+
+        def project(b):
+            banks = []
+            for a in range(CHUNKS):
+                cols = slice(P * a, P * (a + 1))
+                h_t = products.tile([P, PACK, P], F32, tag="p")
+                for s in range(PACK):
+                    nc.tensor.matmul_mx(
+                        out=h_t[:, s, :],
+                        lhsT=w_codes[:, s, :].bitcast(FP8X4),
+                        lhsT_scale=w_scales[:, s, :],
+                        rhs=x1_q[b]["codes"][:, cols].bitcast(FP8X4),
+                        rhs_scale=x1_q[b]["scales"][:, cols],
+                        start=True,
+                        stop=True,
+                    )
+                banks.append(h_t)
+            for a in range(CHUNKS):
+                copy_out_of_psum(
+                    a == 1,
+                    h_q[b]["grouped"][:, P * a : P * (a + 1), :],
+                    banks[a][:].rearrange("p s l -> p l s"),
+                )
+            for a in range(CHUNKS):
+                quantise(h_q[b], slice(P * a, P * (a + 1)))
+
+        def similarity(b):
+            banks = []
+            for a in range(CHUNKS):
+                cols = slice(P * a, P * (a + 1))
+                sim_bank = products.tile([P, L], F32, tag="p")
+                nc.tensor.matmul_mx(
+                    out=sim_bank[:],
+                    lhsT=h_q[b]["codes"][:, cols].bitcast(FP8X4),
+                    lhsT_scale=h_q[b]["scales"][:, cols],
+                    rhs=x2_q[b]["codes"][:].bitcast(FP8X4),
+                    rhs_scale=x2_q[b]["scales"][:],
+                    start=True,
+                    stop=True,
+                )
+                banks.append(sim_bank)
+            out_rows = out[b].rearrange("(p a) m -> p a m", a=CHUNKS)
+            for a in range(CHUNKS):
+                copy_out_of_psum(
+                    a % 2 == 1 if b == B - 1 else a == 1,
+                    sim_rows[b][:, a, :],
+                    banks[a][:].rearrange("p (c m) -> p m c", c=CHUNKS),
+                )
+                nc.sync.dma_start(out=out_rows[:, a, :], in_=sim_rows[b][:, a, :])
+
+        prepare(x1_rows[0], x1_q[0])
+        reorder_w()
+        prepare(x1_rows[1], x1_q[1])
+        project(0)
+        prepare(x2_rows[0], x2_q[0])
+        project(1)
+        prepare(x2_rows[1], x2_q[1])
+        similarity(0)
+        prepare(x1_rows[2], x1_q[2])
+        similarity(1)
+        prepare(x2_rows[2], x2_q[2])
+        project(2)
+        similarity(2)

@@ -24,6 +24,9 @@ SCALE_ROWS = 4
 TRANSPOSE_BANKS = 3
 PRODUCT_BANKS = 5
 
+WARM_COLS = 512
+WARM_MATMULS = 5
+
 FLOPS = 2 * B * L * D * D + 2 * B * L * L * D
 
 
@@ -58,6 +61,8 @@ def tile_coattentionandcombine_pa_kernel(
         w_codes = fixed.tile([P, PACK, P], I32, align_bytes=64)
         ident_f32 = fixed.tile([P, P], F32)
         make_identity(nc, ident_f32[:])
+        zeros = fixed.tile([P, WARM_COLS], BF16)
+        nc.vector.memset(zeros[:], 0.0)
 
         x1_rows, x2_rows, x1_q, x2_q, h_q, sim_rows = [], [], [], [], [], []
         for b in range(B):
@@ -167,6 +172,9 @@ def tile_coattentionandcombine_pa_kernel(
                 )
                 nc.sync.dma_start(out=out_rows[:, a, :], in_=sim_rows[b][:, a, :])
 
+        warm = products.tile([P, WARM_COLS], F32, tag="p")
+        for i in range(WARM_MATMULS):
+            nc.tensor.matmul(warm[:], lhsT=zeros[:, :P], rhs=zeros[:], start=True, stop=True)
         prepare(x1_rows[0], x1_q[0])
         reorder_w()
         prepare(x1_rows[1], x1_q[1])

@@ -21,11 +21,10 @@ WORDS = D // 2
 QUADRANT = 32
 SCALE_ROWS = 4
 
-TRANSPOSE_BANKS = 3
-PRODUCT_BANKS = 5
+BANKS = 8
 
-WARM_COLS = 512
-WARM_MATMULS = 5
+WARM_MATMULS = 8
+WARM_COLS = 256
 
 FLOPS = 2 * B * L * D * D + 2 * B * L * L * D
 
@@ -37,8 +36,7 @@ def tile_coattentionandcombine_pa_kernel(
     with ExitStack() as ctx:
         fixed = ctx.enter_context(tc.tile_pool(name="fixed", bufs=1))
         per_batch = ctx.enter_context(tc.tile_pool(name="per_batch", bufs=B))
-        transposed = ctx.enter_context(tc.psum_pool(name="transposed", bufs=TRANSPOSE_BANKS))
-        products = ctx.enter_context(tc.psum_pool(name="products", bufs=PRODUCT_BANKS))
+        banks = ctx.enter_context(tc.psum_pool(name="banks", bufs=BANKS))
         ctx.enter_context(tc.manual_schedule())
 
         def copy_out_of_psum(on_vector, out_, in_):
@@ -54,6 +52,14 @@ def tile_coattentionandcombine_pa_kernel(
                 in_=operand["grouped"][:, cols, :].rearrange("p l s -> p (l s)"),
             )
 
+        zeros = fixed.tile([P, WARM_COLS], BF16)
+        nc.vector.memset(zeros[:].bitcast(I32), 0)
+        warm = banks.tile([P, L], F32, tag="bank")
+        for i in range(WARM_MATMULS):
+            nc.tensor.matmul(
+                warm[:, :WARM_COLS], lhsT=zeros[:, :P], rhs=zeros[:], start=True, stop=True
+            )
+
         w_scales_in = fixed.tile([P, D], U8, align_bytes=64)
         nc.vector.memset(w_scales_in[:].bitcast(I32), 0)
         w_codes_in = fixed.tile([P, D], I32, align_bytes=64)
@@ -61,8 +67,6 @@ def tile_coattentionandcombine_pa_kernel(
         w_codes = fixed.tile([P, PACK, P], I32, align_bytes=64)
         ident_f32 = fixed.tile([P, P], F32)
         make_identity(nc, ident_f32[:])
-        zeros = fixed.tile([P, WARM_COLS], BF16)
-        nc.vector.memset(zeros[:], 0.0)
 
         x1_rows, x2_rows, x1_q, x2_q, h_q, sim_rows = [], [], [], [], [], []
         for b in range(B):
@@ -77,114 +81,126 @@ def tile_coattentionandcombine_pa_kernel(
             result = per_batch.tile([P, CHUNKS, L], F32, tag="sim_rows")
             sim_rows.append(result)
 
-        def load(tile, tensor, b, pieces):
+        def load_half(tile, tensor, b, half):
+            chunks = slice(HALF // P * half, HALF // P * (half + 1))
             rows = tensor[b].rearrange("(p a) d -> p a d", a=CHUNKS)
-            step = CHUNKS // pieces
-            for a in range(0, CHUNKS, step):
-                nc.sync.dma_start(out=tile[:, a : a + step, :], in_=rows[:, a : a + step, :])
+            nc.sync.dma_start(out=tile[:, chunks, :], in_=rows[:, chunks, :])
 
-        load(x1_rows[0], x1, 0, HALVES)
-        for q in range(P // QUADRANT):
+        def load_w():
+            for q in range(P // QUADRANT):
+                nc.sync.dma_start(
+                    out=w_scales_in[QUADRANT * q : QUADRANT * q + SCALE_ROWS, :].bitcast(I32),
+                    in_=bi_linear_w_scales[0, SCALE_ROWS * q : SCALE_ROWS * (q + 1), :].bitcast(I32),
+                )
             nc.sync.dma_start(
-                out=w_scales_in[QUADRANT * q : QUADRANT * q + SCALE_ROWS, :].bitcast(I32),
-                in_=bi_linear_w_scales[0, SCALE_ROWS * q : SCALE_ROWS * (q + 1), :].bitcast(I32),
+                out=w_codes_in[:], in_=bi_linear_w_words[0].rearrange("p n t -> p (n t)").bitcast(I32)
             )
-        nc.sync.dma_start(
-            out=w_codes_in[:], in_=bi_linear_w_words[0].rearrange("p n t -> p (n t)").bitcast(I32)
-        )
-        load(x1_rows[1], x1, 1, 1)
-        load(x2_rows[0], x2, 0, 1)
-        load(x2_rows[1], x2, 1, 1)
-        load(x1_rows[2], x1, 2, 1)
-        load(x2_rows[2], x2, 2, 1)
 
-
-        def reorder_w():
-            nc.vector.tensor_copy(out=w_codes[:], in_=w_codes_in[:].rearrange("p (m s) -> p s m", s=PACK))
-            nc.vector.tensor_copy(out=w_scales[:], in_=w_scales_in[:].rearrange("p (m s) -> p s m", s=PACK))
-
-        def prepare(rows, operand):
-            banks = []
+        for b in range(B):
             for half in range(HALVES):
-                x_t = transposed.tile([P, PLANES, HALF], F32, tag="t")
-                for a in range(HALF // P):
-                    words = rows[:, HALF // P * half + a, :].bitcast(F32)
-                    for u in range(PLANES):
-                        nc.tensor.transpose(
-                            x_t[:, u, P * a : P * (a + 1)], words[:, u:WORDS:PLANES], ident_f32[:]
-                        )
-                banks.append(x_t)
-            for half in range(HALVES):
-                copy_out_of_psum(
-                    half == 1,
-                    operand["grouped"][:, HALF * half : HALF * (half + 1), :].bitcast(F32),
-                    banks[half][:].rearrange("p u l -> p l u"),
-                )
-            for half in range(HALVES):
-                quantise(operand, slice(HALF * half, HALF * (half + 1)))
+                load_half(x1_rows[b], x1, b, half)
+                load_half(x2_rows[b], x2, b, half)
+                if b == 0 and half == 0:
+                    load_w()
 
-        def project(b):
-            banks = []
-            for a in range(CHUNKS):
-                cols = slice(P * a, P * (a + 1))
-                h_t = products.tile([P, PACK, P], F32, tag="p")
-                for s in range(PACK):
-                    nc.tensor.matmul_mx(
-                        out=h_t[:, s, :],
-                        lhsT=w_codes[:, s, :].bitcast(FP8X4),
-                        lhsT_scale=w_scales[:, s, :],
-                        rhs=x1_q[b]["codes"][:, cols].bitcast(FP8X4),
-                        rhs_scale=x1_q[b]["scales"][:, cols],
-                        start=True,
-                        stop=True,
+        def columns(first, count):
+            return slice(P * first, P * (first + count))
+
+        def transpose_half(rows, half):
+            bank = banks.tile([P, PLANES, HALF], F32, tag="bank")
+            for a in range(HALF // P):
+                words = rows[:, HALF // P * half + a, :].bitcast(F32)
+                for u in range(PLANES):
+                    nc.tensor.transpose(
+                        bank[:, u, P * a : P * (a + 1)], words[:, u:WORDS:PLANES], ident_f32[:]
                     )
-                banks.append(h_t)
-            for a in range(CHUNKS):
-                copy_out_of_psum(
-                    a == 1,
-                    h_q[b]["grouped"][:, P * a : P * (a + 1), :],
-                    banks[a][:].rearrange("p s l -> p l s"),
-                )
-            for a in range(CHUNKS):
-                quantise(h_q[b], slice(P * a, P * (a + 1)))
+            return bank
 
-        def similarity(b):
-            banks = []
-            for a in range(CHUNKS):
-                cols = slice(P * a, P * (a + 1))
-                sim_bank = products.tile([P, L], F32, tag="p")
+        def project_chunk(b, a):
+            bank = banks.tile([P, PACK, P], F32, tag="bank")
+            for s in range(PACK):
                 nc.tensor.matmul_mx(
-                    out=sim_bank[:],
-                    lhsT=h_q[b]["codes"][:, cols].bitcast(FP8X4),
-                    lhsT_scale=h_q[b]["scales"][:, cols],
-                    rhs=x2_q[b]["codes"][:].bitcast(FP8X4),
-                    rhs_scale=x2_q[b]["scales"][:],
+                    out=bank[:, s, :],
+                    lhsT=w_codes[:, s, :].bitcast(FP8X4),
+                    lhsT_scale=w_scales[:, s, :],
+                    rhs=x1_q[b]["codes"][:, columns(a, 1)].bitcast(FP8X4),
+                    rhs_scale=x1_q[b]["scales"][:, columns(a, 1)],
                     start=True,
                     stop=True,
                 )
-                banks.append(sim_bank)
-            out_rows = out[b].rearrange("(p a) m -> p a m", a=CHUNKS)
-            for a in range(CHUNKS):
-                copy_out_of_psum(
-                    a % 2 == 1 if b == B - 1 else a == 1,
-                    sim_rows[b][:, a, :],
-                    banks[a][:].rearrange("p (c m) -> p m c", c=CHUNKS),
-                )
-                nc.sync.dma_start(out=out_rows[:, a, :], in_=sim_rows[b][:, a, :])
+            return bank
 
-        warm = products.tile([P, WARM_COLS], F32, tag="p")
-        for i in range(WARM_MATMULS):
-            nc.tensor.matmul(warm[:], lhsT=zeros[:, :P], rhs=zeros[:], start=True, stop=True)
-        prepare(x1_rows[0], x1_q[0])
-        reorder_w()
-        prepare(x1_rows[1], x1_q[1])
-        project(0)
-        prepare(x2_rows[0], x2_q[0])
-        project(1)
-        prepare(x2_rows[1], x2_q[1])
-        similarity(0)
-        prepare(x1_rows[2], x1_q[2])
-        similarity(1)
-        prepare(x2_rows[2], x2_q[2])
-        project(2)
-        similarity(2)
+        def similarity_chunk(b, a):
+            bank = banks.tile([P, L], F32, tag="bank")
+            nc.tensor.matmul_mx(
+                out=bank[:],
+                lhsT=h_q[b]["codes"][:, columns(a, 1)].bitcast(FP8X4),
+                lhsT_scale=h_q[b]["scales"][:, columns(a, 1)],
+                rhs=x2_q[b]["codes"][:].bitcast(FP8X4),
+                rhs_scale=x2_q[b]["scales"][:],
+                start=True,
+                stop=True,
+            )
+            return bank
+
+        def reorder_w():
+            nc.vector.tensor_copy(out=w_scales[:], in_=w_scales_in[:].rearrange("p (m s) -> p s m", s=PACK))
+            nc.vector.tensor_copy(out=w_codes[:], in_=w_codes_in[:].rearrange("p (m s) -> p s m", s=PACK))
+
+        def run(units):
+            for kind, b, i, on_vector in units:
+                if kind == "x1" or kind == "x2":
+                    operand = x1_q[b] if kind == "x1" else x2_q[b]
+                    bank = transpose_half(x1_rows[b] if kind == "x1" else x2_rows[b], i)
+                    cols = columns(HALF // P * i, HALF // P)
+                    copy_out_of_psum(
+                        on_vector,
+                        operand["grouped"][:, cols, :].bitcast(F32),
+                        bank[:].rearrange("p u l -> p l u"),
+                    )
+                    pending.append((operand, cols))
+                elif kind == "h":
+                    bank = project_chunk(b, i)
+                    cols = columns(i, 1)
+                    copy_out_of_psum(
+                        on_vector, h_q[b]["grouped"][:, cols, :], bank[:].rearrange("p s l -> p l s")
+                    )
+                    pending.append((h_q[b], cols))
+                else:
+                    bank = similarity_chunk(b, i)
+                    copy_out_of_psum(
+                        on_vector,
+                        sim_rows[b][:, i, :],
+                        bank[:].rearrange("p (c m) -> p m c", c=CHUNKS),
+                    )
+                    nc.sync.dma_start(
+                        out=out[b].rearrange("(p a) m -> p a m", a=CHUNKS)[:, i, :],
+                        in_=sim_rows[b][:, i, :],
+                    )
+
+        def quantise_pending(leave):
+            while len(pending) > leave:
+                operand, cols = pending[0]
+                pending.remove(pending[0])
+                quantise(operand, cols)
+
+        pending = []
+        halves = [(b, half) for b in range(B) for half in range(HALVES)]
+
+        def half_chunks(half):
+            return range(HALF // P * half, HALF // P * (half + 1))
+
+        def run_group(units):
+            run(units)
+            quantise_pending(len([u for u in units if u[0] != "sim"]))
+
+        for step in range(len(halves) + 3):
+            for kind, delay in (("x1", 0), ("x2", 0), ("h", 1), ("sim", 3)):
+                if 0 <= step - delay < len(halves):
+                    b, half = halves[step - delay]
+                    if kind == "x1" and step == 1:
+                        reorder_w()
+                    if kind == "x1" or kind == "x2":
+                        run_group([(kind, b, half, False)])
+                    else:
+                        run_group([(kind, b, a, a % 2 == 0) for a in half_chunks(half)])

@@ -148,6 +148,7 @@ def tile_coattentionandcombine_pa_kernel(
             nc.vector.tensor_copy(out=w_codes[:], in_=w_codes_in[:].rearrange("p (m s) -> p s m", s=PACK))
 
         def run(units):
+            operand, cols = None, None
             for kind, b, i, on_vector in units:
                 if kind == "x1" or kind == "x2":
                     operand = x1_q[b] if kind == "x1" else x2_q[b]
@@ -158,14 +159,14 @@ def tile_coattentionandcombine_pa_kernel(
                         operand["grouped"][:, cols, :].bitcast(F32),
                         bank[:].rearrange("p u l -> p l u"),
                     )
-                    pending.append((operand, cols))
                 elif kind == "h":
                     bank = project_chunk(b, i)
-                    cols = columns(i, 1)
+                    operand, cols = h_q[b], columns(i // 2 * 2, 2)
                     copy_out_of_psum(
-                        on_vector, h_q[b]["grouped"][:, cols, :], bank[:].rearrange("p s l -> p l s")
+                        on_vector,
+                        operand["grouped"][:, columns(i, 1), :],
+                        bank[:].rearrange("p s l -> p l s"),
                     )
-                    pending.append((h_q[b], cols))
                 else:
                     bank = similarity_chunk(b, i)
                     copy_out_of_psum(
@@ -177,30 +178,36 @@ def tile_coattentionandcombine_pa_kernel(
                         out=out[b].rearrange("(p a) m -> p a m", a=CHUNKS)[:, i, :],
                         in_=sim_rows[b][:, i, :],
                     )
+            return (operand, cols)
 
-        def quantise_pending(leave):
-            while len(pending) > leave:
-                operand, cols = pending[0]
-                pending.remove(pending[0])
-                quantise(operand, cols)
-
-        pending = []
         halves = [(b, half) for b in range(B) for half in range(HALVES)]
 
         def half_chunks(half):
             return range(HALF // P * half, HALF // P * (half + 1))
 
-        def run_group(units):
-            run(units)
-            quantise_pending(len([u for u in units if u[0] != "sim"]))
-
+        last = len(halves) - 1
+        to_quantise = None
         for step in range(len(halves) + 3):
             for kind, delay in (("x1", 0), ("x2", 0), ("h", 1), ("sim", 3)):
-                if 0 <= step - delay < len(halves):
-                    b, half = halves[step - delay]
+                j = step - delay
+                if 0 <= j <= last:
+                    b, half = halves[j]
                     if kind == "x1" and step == 1:
                         reorder_w()
                     if kind == "x1" or kind == "x2":
-                        run_group([(kind, b, half, False)])
+                        done = run([(kind, b, half, False)])
                     else:
-                        run_group([(kind, b, a, a % 2 == 0) for a in half_chunks(half)])
+                        done = run(
+                            [
+                                (kind, b, a, a % 2 == 1 and (kind == "h" or step != last + 1))
+                                for a in half_chunks(half)
+                            ]
+                        )
+                    if to_quantise is not None:
+                        operand, cols = to_quantise
+                        if step <= last:
+                            quantise(operand, cols)
+                        else:
+                            quantise(operand, slice(cols.start, cols.start + P))
+                            quantise(operand, slice(cols.start + P, cols.stop))
+                    to_quantise = None if kind == "sim" else done

@@ -192,7 +192,7 @@ def tile_coattentionandcombine_pa_kernel(
                 j = step - delay
                 if 0 <= j <= last:
                     b, half = halves[j]
-                    if kind == "x1" and step == 1:
+                    if kind == "x2" and step == 0:
                         reorder_w()
                     if kind == "x1" or kind == "x2":
                         done = run([(kind, b, half, False)])

@@ -54,11 +54,14 @@ def tile_coattentionandcombine_pa_kernel(
 
         zeros = fixed.tile([P, WARM_COLS], BF16)
         nc.vector.memset(zeros[:].bitcast(I32), 0)
-        warm = banks.tile([P, L], F32, tag="bank")
-        for i in range(WARM_MATMULS):
-            nc.tensor.matmul(
-                warm[:, :WARM_COLS], lhsT=zeros[:, :P], rhs=zeros[:], start=True, stop=True
-            )
+        def warm_up(matmuls):
+            warm = banks.tile([P, L], F32, tag="bank")
+            for i in range(matmuls):
+                nc.tensor.matmul(
+                    warm[:, :WARM_COLS], lhsT=zeros[:, :P], rhs=zeros[:], start=True, stop=True
+                )
+
+        warm_up(WARM_MATMULS)
 
         w_scales_in = fixed.tile([P, D], U8, align_bytes=64)
         nc.vector.memset(w_scales_in[:].bitcast(I32), 0)
@@ -188,7 +191,8 @@ def tile_coattentionandcombine_pa_kernel(
         last = len(halves) - 1
         to_quantise = None
         for step in range(len(halves) + 3):
-            for kind, delay in (("x1", 0), ("x2", 0), ("h", 1), ("sim", 3)):
+            order = (("x1", 0), ("h", 1), ("x2", 0)) if step == 1 else (("x1", 0), ("x2", 0), ("h", 1), ("sim", 3))
+            for kind, delay in order:
                 j = step - delay
                 if 0 <= j <= last:
                     b, half = halves[j]
@@ -196,6 +200,8 @@ def tile_coattentionandcombine_pa_kernel(
                         reorder_w()
                     if kind == "x1" or kind == "x2":
                         done = run([(kind, b, half, False)])
+                        if kind == "x2" and step == 0:
+                            warm_up(3)
                     else:
                         done = run(
                             [

from contextlib import ExitStack

import concourse.mybir as mybir
from concourse.masks import make_identity

BF16 = mybir.dt.bfloat16
F32 = mybir.dt.float32
I32 = mybir.dt.int32
U32 = mybir.dt.uint32
U8 = mybir.dt.uint8
FP8X4 = mybir.dt.float8_e4m3fn_x4

B, L, D = 3, 512, 512
P = 128
PACK = 4
CHUNKS = L // P
HALF = L // 2
HALVES = L // HALF
PLANES = 2
WORDS = D // 2
QUADRANT = 32
SCALE_ROWS = 4

BANKS = 8

WARM_MATMULS = 8
WARM_COLS = 256

FLOPS = 2 * B * L * D * D + 2 * B * L * L * D


def tile_coattentionandcombine_pa_kernel(
    tc, x1, bi_linear_w_words, bi_linear_w_scales, x2, out
):
    nc = tc.nc
    with ExitStack() as ctx:
        fixed = ctx.enter_context(tc.tile_pool(name="fixed", bufs=1))
        per_batch = ctx.enter_context(tc.tile_pool(name="per_batch", bufs=B))
        banks = ctx.enter_context(tc.psum_pool(name="banks", bufs=BANKS))
        ctx.enter_context(tc.manual_schedule())

        def copy_out_of_psum(on_vector, out_, in_):
            if on_vector:
                nc.vector.tensor_copy(out=out_, in_=in_)
            else:
                nc.scalar.copy(out=out_, in_=in_)

        def quantise(operand, cols):
            nc.vector.quantize_mx(
                out=operand["codes"][:, cols].bitcast(FP8X4),
                scales=operand["scales"][:, cols],
                in_=operand["grouped"][:, cols, :].rearrange("p l s -> p (l s)"),
            )

        zeros = fixed.tile([P, WARM_COLS], BF16)
        nc.vector.memset(zeros[:].bitcast(I32), 0)
        def warm_up(matmuls):
            warm = banks.tile([P, L], F32, tag="bank")
            for i in range(matmuls):
                nc.tensor.matmul(
                    warm[:, :WARM_COLS], lhsT=zeros[:, :P], rhs=zeros[:], start=True, stop=True
                )

        warm_up(WARM_MATMULS)

        w_scales_in = fixed.tile([P, D], U8, align_bytes=64)
        nc.vector.memset(w_scales_in[:].bitcast(I32), 0)
        w_codes_in = fixed.tile([P, D], I32, align_bytes=64)
        w_scales = fixed.tile([P, PACK, P], U8, align_bytes=64)
        w_codes = fixed.tile([P, PACK, P], I32, align_bytes=64)
        ident_f32 = fixed.tile([P, P], F32)
        make_identity(nc, ident_f32[:])

        x1_rows, x2_rows, x1_q, x2_q, h_q, sim_rows = [], [], [], [], [], []
        for b in range(B):
            for rows_of, name in ((x1_rows, "x1_rows"), (x2_rows, "x2_rows")):
                rows = per_batch.tile([P, CHUNKS, D], BF16, tag=name)
                rows_of.append(rows)
            for operands, name in ((x1_q, "x1"), (x2_q, "x2"), (h_q, "h")):
                grouped = per_batch.tile([P, L, PACK], BF16, align_bytes=64, tag=name + "_grouped")
                codes = per_batch.tile([P, L], U32, align_bytes=64, tag=name + "_codes")
                scales = per_batch.tile([P, L], U8, align_bytes=64, tag=name + "_scales")
                operands.append({"grouped": grouped, "codes": codes, "scales": scales})
            result = per_batch.tile([P, CHUNKS, L], F32, tag="sim_rows")
            sim_rows.append(result)

        def load_half(tile, tensor, b, half):
            chunks = slice(HALF // P * half, HALF // P * (half + 1))
            rows = tensor[b].rearrange("(p a) d -> p a d", a=CHUNKS)
            nc.sync.dma_start(out=tile[:, chunks, :], in_=rows[:, chunks, :])

        def load_w():
            for q in range(P // QUADRANT):
                nc.sync.dma_start(
                    out=w_scales_in[QUADRANT * q : QUADRANT * q + SCALE_ROWS, :].bitcast(I32),
                    in_=bi_linear_w_scales[0, SCALE_ROWS * q : SCALE_ROWS * (q + 1), :].bitcast(I32),
                )
            nc.sync.dma_start(
                out=w_codes_in[:], in_=bi_linear_w_words[0].rearrange("p n t -> p (n t)").bitcast(I32)
            )

        for b in range(B):
            for half in range(HALVES):
                load_half(x1_rows[b], x1, b, half)
                load_half(x2_rows[b], x2, b, half)
                if b == 0 and half == 0:
                    load_w()

        def columns(first, count):
            return slice(P * first, P * (first + count))

        def transpose_half(rows, half):
            bank = banks.tile([P, PLANES, HALF], F32, tag="bank")
            for a in range(HALF // P):
                words = rows[:, HALF // P * half + a, :].bitcast(F32)
                for u in range(PLANES):
                    nc.tensor.transpose(
                        bank[:, u, P * a : P * (a + 1)], words[:, u:WORDS:PLANES], ident_f32[:]
                    )
            return bank

        def project_chunk(b, a):
            bank = banks.tile([P, PACK, P], F32, tag="bank")
            for s in range(PACK):
                nc.tensor.matmul_mx(
                    out=bank[:, s, :],
                    lhsT=w_codes[:, s, :].bitcast(FP8X4),
                    lhsT_scale=w_scales[:, s, :],
                    rhs=x1_q[b]["codes"][:, columns(a, 1)].bitcast(FP8X4),
                    rhs_scale=x1_q[b]["scales"][:, columns(a, 1)],
                    start=True,
                    stop=True,
                )
            return bank

        def similarity_chunk(b, a):
            bank = banks.tile([P, L], F32, tag="bank")
            nc.tensor.matmul_mx(
                out=bank[:],
                lhsT=h_q[b]["codes"][:, columns(a, 1)].bitcast(FP8X4),
                lhsT_scale=h_q[b]["scales"][:, columns(a, 1)],
                rhs=x2_q[b]["codes"][:].bitcast(FP8X4),
                rhs_scale=x2_q[b]["scales"][:],
                start=True,
                stop=True,
            )
            return bank

        def reorder_w():
            nc.vector.tensor_copy(out=w_scales[:], in_=w_scales_in[:].rearrange("p (m s) -> p s m", s=PACK))
            nc.vector.tensor_copy(out=w_codes[:], in_=w_codes_in[:].rearrange("p (m s) -> p s m", s=PACK))

        def run(units):
            operand, cols = None, None
            for kind, b, i, on_vector in units:
                if kind == "x1" or kind == "x2":
                    operand = x1_q[b] if kind == "x1" else x2_q[b]
                    bank = transpose_half(x1_rows[b] if kind == "x1" else x2_rows[b], i)
                    cols = columns(HALF // P * i, HALF // P)
                    copy_out_of_psum(
                        on_vector,
                        operand["grouped"][:, cols, :].bitcast(F32),
                        bank[:].rearrange("p u l -> p l u"),
                    )
                elif kind == "h":
                    bank = project_chunk(b, i)
                    operand, cols = h_q[b], columns(i // 2 * 2, 2)
                    copy_out_of_psum(
                        on_vector,
                        operand["grouped"][:, columns(i, 1), :],
                        bank[:].rearrange("p s l -> p l s"),
                    )
                else:
                    bank = similarity_chunk(b, i)
                    copy_out_of_psum(
                        on_vector,
                        sim_rows[b][:, i, :],
                        bank[:].rearrange("p (c m) -> p m c", c=CHUNKS),
                    )
                    nc.sync.dma_start(
                        out=out[b].rearrange("(p a) m -> p a m", a=CHUNKS)[:, i, :],
                        in_=sim_rows[b][:, i, :],
                    )
            return (operand, cols)

        halves = [(b, half) for b in range(B) for half in range(HALVES)]

        def half_chunks(half):
            return range(HALF // P * half, HALF // P * (half + 1))

        last = len(halves) - 1
        to_quantise = None
        for step in range(len(halves) + 3):
            order = (("x1", 0), ("h", 1), ("x2", 0)) if step == 1 else (("x1", 0), ("x2", 0), ("h", 1), ("sim", 3))
            for kind, delay in order:
                j = step - delay
                if 0 <= j <= last:
                    b, half = halves[j]
                    if kind == "x2" and step == 0:
                        reorder_w()
                    if kind == "x1" or kind == "x2":
                        done = run([(kind, b, half, False)])
                        if kind == "x2" and step == 0:
                            warm_up(3)
                    else:
                        done = run(
                            [
                                (kind, b, a, a % 2 == 1 and (kind == "h" or step != last + 1))
                                for a in half_chunks(half)
                            ]
                        )
                    if to_quantise is not None:
                        operand, cols = to_quantise
                        if step <= last:
                            quantise(operand, cols)
                        else:
                            quantise(operand, slice(cols.start, cols.start + P))
                            quantise(operand, slice(cols.start + P, cols.stop))
                    to_quantise = None if kind == "sim" else done
